import numpy as np
import ml_dtypes


def mxq(x, axis, fmt="e4m3"):
    dtype, down = {"e4m3": (ml_dtypes.float8_e4m3fn, 7), "e5m2": (ml_dtypes.float8_e5m2, 14)}[fmt]
    v = np.moveaxis(np.asarray(x, np.float32).astype(ml_dtypes.bfloat16).astype(np.float64), axis, -1)
    blocks = v.reshape(v.shape[:-1] + (-1, 32))
    amax = np.abs(blocks).max(-1, keepdims=True)
    byte = np.maximum(np.where(amax > 0, np.frexp(amax)[1] - 1 + 127, 0) - down, 1)
    scale = np.exp2(byte - 127.0)
    codes = (blocks / scale).astype(np.float32).astype(dtype).astype(np.float64)
    return np.moveaxis((codes * scale).reshape(v.shape), -1, axis)


WIDE = False


def mx_kscale(k):
    if not WIDE:
        return np.ones(k)
    levels = np.array([10, -10, 5, -5, 0])
    a = np.random.permutation(np.resize(levels, k // 512 * 4)).reshape(k // 512, 4)
    idx = np.arange(k)
    return np.exp2(a[idx // 512, idx % 128 // 32])


BF16 = ml_dtypes.bfloat16


def bf(x):
    return np.asarray(x, np.float32).astype(BF16)


def f64(x):
    return np.asarray(x).astype(np.float64)


B, DIM, E, HID = 1024, 1024, 1024, 2048
EPS = 1e-5


def layer_norm(y, g, b):
    m = y.mean(-1, keepdims=True)
    v = ((y - m) ** 2).mean(-1, keepdims=True)
    return (y - m) / np.sqrt(v + EPS) * g + b


def setup_inputs():
    s, t = mx_kscale(DIM), mx_kscale(E)
    r = np.random.standard_normal
    return {'feat': bf(r((B, DIM))),
            'own_self': bf(r((B, DIM))),
            'other_self': bf(r((B, DIM)) * s),
            'Wv': bf(r((E, DIM)) / np.sqrt(DIM) / s[None, :] * t[:, None]),
            'bv': bf(r(E) * 0.2 * t),
            'Wo': bf(r((DIM, E)) / np.sqrt(E) / t[None, :]),
            'bo': bf(r(DIM) * 0.2),
            'g': bf(1.0 + 0.1 * r(DIM)),
            'be': bf(0.1 * r(DIM))}


def reference(feat, own_self, other_self, Wv, bv, Wo, bo, g, be):
    val = (mxq(f64(other_self), 1, 'e4m3') @ mxq(f64(Wv), 1, 'e4m3').T) + f64(bv)
    cross = (mxq(val, 1, 'e4m3') @ mxq(f64(Wo), 1, 'e4m3').T) + f64(bo)
    return layer_norm(f64(feat) + (f64(own_self) + cross) * 0.5, f64(g), f64(be))

@@ -1,0 +1,284 @@
+from contextlib import ExitStack
+
+import concourse.mybir as mybir
+from concourse.masks import make_identity
+
+BF16 = mybir.dt.bfloat16
+F32 = mybir.dt.float32
+U32 = mybir.dt.uint32
+U8 = mybir.dt.uint8
+FP8X4 = mybir.dt.float8_e4m3fn_x4
+ACT = mybir.ActivationFunctionType
+ALU = mybir.AluOpType
+
+P = 128
+SIZE = 1024
+PACK = 4
+PASSES = SIZE // (P * PACK)
+TILES = SIZE // P
+PAIRS = TILES // 2
+HALF = 512
+HALF_TILES = HALF // P
+BANK_BLOCKS = HALF // P
+EPS = 1e-5
+
+FLOPS = 2 * 2 * SIZE * SIZE * SIZE
+
+
+def tile_efficientfusionlayer_pb_kernel(
+    tc, feat, own_self, other_self, Wv, bv, Wo, bo, g, be, out
+):
+    nc = tc.nc
+
+    x_view = other_self.rearrange("(p j e) d -> p j e d", j=PAIRS, e=2)
+    feat_view = feat.rearrange("(p j e) d -> p j e d", j=PAIRS, e=2)
+    own_view = own_self.rearrange("(p j e) d -> p j e d", j=PAIRS, e=2)
+    out_view = out.rearrange("(p t) d -> p t d", t=TILES)
+    wv_view = Wv.rearrange("(j p e) d -> p j e d", j=PAIRS, e=2)
+    bv_view = bv.rearrange("(j p e) -> p j e", j=PAIRS, e=2)
+    wo_view = Wo.rearrange("(j e p) v -> p j e v", j=PAIRS, e=2)
+    bo_view = bo.rearrange("(i p) -> p i", p=P)
+
+    with ExitStack() as pools:
+        const = pools.enter_context(tc.tile_pool(name="const", bufs=1))
+        keep = pools.enter_context(tc.tile_pool(name="keep", bufs=1))
+        weight_rows = pools.enter_context(tc.tile_pool(name="weight_rows", bufs=6))
+        resid_rows = pools.enter_context(tc.tile_pool(name="resid_rows", bufs=4))
+        stage_one = pools.enter_context(tc.tile_pool(name="stage_one", bufs=4))
+        stage_half = pools.enter_context(tc.tile_pool(name="stage_half", bufs=1))
+        work = pools.enter_context(tc.tile_pool(name="work", bufs=2))
+        normed = pools.enter_context(tc.tile_pool(name="normed", bufs=3))
+        small = pools.enter_context(tc.tile_pool(name="small", bufs=3))
+        psum_chain = pools.enter_context(tc.psum_pool(name="psum_chain", bufs=4))
+        psum_back = pools.enter_context(tc.psum_pool(name="psum_back", bufs=4))
+
+        ident = const.tile([P, P], F32)
+        make_identity(nc, ident[:])
+        eps_col = const.tile([P, 1], F32)
+        nc.vector.memset(eps_col[:], EPS)
+        warm = const.tile([P, 1], F32)
+        nc.scalar.activation(out=warm[:], in_=eps_col[:], func=ACT.Sqrt)
+
+        bv_raw = const.tile([P, TILES], BF16)
+        nc.scalar.dma_start(out=bv_raw[:].rearrange("p (j e) -> p j e", e=2), in_=bv_view)
+        bo_raw = const.tile([P, TILES], BF16)
+        with nc.allow_non_contiguous_dma(reason="1024 bias values, one to a partition"):
+            nc.scalar.dma_start(out=bo_raw[:], in_=bo_view)
+        bv_col = const.tile([P, TILES], F32)
+        nc.vector.tensor_copy(out=bv_col[:], in_=bv_raw[:])
+        bo_col = const.tile([P, TILES], F32)
+        nc.vector.tensor_copy(out=bo_col[:], in_=bo_raw[:])
+
+        def load_pair(pool, view, j):
+            rows = pool.tile([P, 2, SIZE], BF16, tag="rows")
+            nc.sync.dma_start(out=rows[:], in_=view[:, j])
+            return rows
+
+        def quantise_transposed(stage, row_tiles, name):
+            n_rows = P * len(row_tiles)
+            grouped = stage.tile([P, PASSES, n_rows, PACK], BF16, tag="grouped", align_bytes=64)
+            grouped_words = grouped[:].bitcast(F32)
+            for n, rows in enumerate(row_tiles):
+                words = rows.bitcast(F32)
+                turned = psum_chain.tile([P, PASSES, 2, P], F32, tag="chain")
+                for c in range(PASSES):
+                    for u in range(2):
+                        first = (2 * c + u) * P
+                        nc.tensor.transpose(turned[:, c, u, :], words[:, first : first + P], ident[:])
+                nc.scalar.copy(
+                    out=grouped_words[:, :, n * P : (n + 1) * P, :],
+                    in_=turned[:].rearrange("p c u r -> p c r u"),
+                )
+            codes = keep.tile([P, PASSES, n_rows], U32, name=name + "_codes", align_bytes=64)
+            scales = keep.tile([P, PASSES, n_rows], U8, name=name + "_scales", align_bytes=64)
+            nc.vector.quantize_mx(
+                out=codes[:].rearrange("p c r -> p (c r)").bitcast(FP8X4),
+                scales=scales[:].rearrange("p c r -> p (c r)"),
+                in_=grouped[:].rearrange("p c r t -> p (c r t)"),
+            )
+            return codes, scales
+
+        def mx_product(acc, stationary, moving):
+            for c in range(PASSES):
+                nc.tensor.matmul_mx(
+                    out=acc,
+                    lhsT=stationary[0][:, c, :].bitcast(FP8X4),
+                    lhsT_scale=stationary[1][:, c, :],
+                    rhs=moving[0][:, c, :].bitcast(FP8X4),
+                    rhs_scale=moving[1][:, c, :],
+                    start=(c == 0),
+                    stop=(c == PASSES - 1),
+                )
+
+        def quantise_weight(view, name):
+            quantised = []
+            for j in range(PAIRS):
+                rows = load_pair(weight_rows, view, j)
+                for e in range(2):
+                    tile_name = "%s%d" % (name, 2 * j + e)
+                    quantised.append(quantise_transposed(stage_one, [rows[:, e, :]], tile_name))
+            return quantised
+
+        def quantise_batch_half(h):
+            pairs = [load_pair(weight_rows, x_view, 2 * h + k) for k in range(2)]
+            row_tiles = [rows[:, e, :] for rows in pairs for e in range(2)]
+            return quantise_transposed(stage_half, row_tiles, "x%d" % h)
+
+        def value_pass(x_q, val_q, c):
+            planes = work.tile([P, PACK, HALF], BF16, tag="planes")
+            for t in range(PACK):
+                acc = psum_chain.tile([P, HALF], F32, tag="chain")
+                mx_product(acc[:], wv_q[PACK * c + t], x_q)
+                nc.scalar.activation(
+                    out=planes[:, t, :],
+                    in_=acc[:],
+                    func=ACT.Identity,
+                    bias=bv_col[:, PACK * c + t : PACK * c + t + 1],
+                    scale=1.0,
+                )
+            grouped = work.tile([P, HALF, PACK], BF16, tag="val_grouped", align_bytes=64)
+            nc.vector.tensor_copy(
+                out=grouped[:].rearrange("p (n i) t -> p n t i", i=4),
+                in_=planes[:].rearrange("p t (n i) -> p n t i", i=4),
+            )
+            nc.vector.quantize_mx(
+                out=val_q[0][:, c, :].bitcast(FP8X4),
+                scales=val_q[1][:, c, :],
+                in_=grouped[:].rearrange("p n t -> p (n t)"),
+            )
+
+        def new_val(h):
+            codes = keep.tile([P, PASSES, HALF], U32, name="val%d_codes" % h, align_bytes=64)
+            scales = keep.tile([P, PASSES, HALF], U8, name="val%d_scales" % h, align_bytes=64)
+            return codes, scales
+
+        def cross_transposed(val_q, h):
+            cross_t = keep.tile([P, TILES, HALF], F32, name="cross_t%d" % h)
+            for i in range(TILES):
+                acc = psum_chain.tile([P, HALF], F32, tag="chain")
+                mx_product(acc[:], wo_q[i], val_q)
+                nc.scalar.activation(
+                    out=cross_t[:, i, :],
+                    in_=acc[:],
+                    func=ACT.Identity,
+                    bias=bo_col[:, i : i + 1],
+                    scale=1.0,
+                )
+            return cross_t
+
+        y = []
+
+        def residual_pair(j):
+            feat_rows = load_pair(resid_rows, feat_view, j)
+            own_rows = load_pair(resid_rows, own_view, j)
+            for e in range(2):
+                y_tile = keep.tile([P, SIZE], F32, name="y%d" % (2 * j + e))
+                nc.vector.scalar_tensor_tensor(
+                    out=y_tile[:],
+                    in0=own_rows[:, e, :],
+                    scalar=0.5,
+                    in1=feat_rows[:, e, :],
+                    op0=ALU.mult,
+                    op1=ALU.add,
+                )
+                y.append(y_tile)
+
+        def centre(t, cross_t):
+            first = (t % HALF_TILES) * P
+            sums = small.tile([P, 2], F32, tag="sums")
+            for k in range(2):
+                back = psum_back.tile([P, BANK_BLOCKS, P], F32, tag="back")
+                for n in range(BANK_BLOCKS):
+                    nc.tensor.transpose(
+                        back[:, n, :], cross_t[:, BANK_BLOCKS * k + n, first : first + P], ident[:]
+                    )
+                cols = slice(k * HALF, (k + 1) * HALF)
+                nc.vector.scalar_tensor_tensor(
+                    out=y[t][:, cols],
+                    in0=back[:].rearrange("p n r -> p (n r)"),
+                    scalar=0.5,
+                    in1=y[t][:, cols],
+                    op0=ALU.mult,
+                    op1=ALU.add,
+                    accum_out=sums[:, k : k + 1],
+                )
+            neg_mean = small.tile([P, 1], F32, tag="neg_mean")
+            nc.vector.tensor_scalar(
+                out=neg_mean[:],
+                in0=sums[:, 0:1],
+                scalar1=sums[:, 1:2],
+                scalar2=-1.0 / SIZE,
+                op0=ALU.add,
+                op1=ALU.mult,
+            )
+            squares = work.tile([P, SIZE], BF16, tag="squares")
+            sum_sq = small.tile([P, 1], F32, tag="sum_sq")
+            nc.scalar.activation(
+                out=squares[:],
+                in_=y[t][:],
+                func=ACT.Square,
+                bias=neg_mean[:],
+                scale=1.0,
+                accum_out=sum_sq[:],
+            )
+            std = small.tile([P, 1], F32, tag="std")
+            nc.scalar.activation(
+                out=std[:], in_=sum_sq[:], func=ACT.Sqrt, bias=eps_col[:], scale=1.0 / SIZE
+            )
+            result = normed.tile([P, SIZE], F32, tag="result")
+            nc.vector.scalar_tensor_tensor(
+                out=result[:],
+                in0=y[t][:],
+                scalar=neg_mean[:],
+                in1=g_all[:],
+                op0=ALU.add,
+                op1=ALU.mult,
+            )
+            return result, std
+
+        def finish(t, centred):
+            result, std = centred
+            rstd = small.tile([P, 1], F32, tag="rstd")
+            nc.vector.reciprocal(out=rstd[:], in_=std[:])
+            nc.vector.scalar_tensor_tensor(
+                out=result[:],
+                in0=result[:],
+                scalar=rstd[:],
+                in1=be_all[:],
+                op0=ALU.mult,
+                op1=ALU.add,
+            )
+            nc.sync.dma_start(out=out_view[:, t, :], in_=result[:])
+
+        x_q0 = quantise_batch_half(0)
+        wv_q = quantise_weight(wv_view, "wv")
+        val_q0 = new_val(0)
+        for c in range(PASSES):
+            value_pass(x_q0, val_q0, c)
+        wo_q = quantise_weight(wo_view, "wo")
+        g_all = const.tile([P, SIZE], BF16)
+        nc.sync.dma_start(out=g_all[:], in_=g.partition_broadcast(P))
+        be_all = const.tile([P, SIZE], BF16)
+        nc.sync.dma_start(out=be_all[:], in_=be.partition_broadcast(P))
+        residual_pair(0)
+        residual_pair(1)
+        cross_t0 = cross_transposed(val_q0, 0)
+
+        x_q1 = quantise_batch_half(1)
+        residual_pair(2)
+        residual_pair(3)
+        val_q1 = new_val(1)
+        centred = centre(0, cross_t0)
+        value_pass(x_q1, val_q1, 0)
+        previous, centred = centred, centre(1, cross_t0)
+        finish(0, previous)
+        value_pass(x_q1, val_q1, 1)
+        previous, centred = centred, centre(2, cross_t0)
+        finish(1, previous)
+        cross_t1 = cross_transposed(val_q1, 1)
+        previous, centred = centred, centre(3, cross_t0)
+        finish(2, previous)
+        for t in range(HALF_TILES, TILES):
+            previous, centred = centred, centre(t, cross_t1)
+            finish(t - 1, previous)
+        finish(TILES - 1, centred)

@@ -5,6 +5,7 @@ from concourse.masks import make_identity
 
 BF16 = mybir.dt.bfloat16
 F32 = mybir.dt.float32
+I32 = mybir.dt.int32
 U32 = mybir.dt.uint32
 U8 = mybir.dt.uint8
 FP8X4 = mybir.dt.float8_e4m3fn_x4
@@ -20,6 +21,7 @@ PAIRS = TILES // 2
 HALF = 512
 HALF_TILES = HALF // P
 BANK_BLOCKS = HALF // P
+VECTOR_TURN = 4
 EPS = 1e-5
 
 FLOPS = 2 * 2 * SIZE * SIZE * SIZE
@@ -40,10 +42,10 @@ def tile_efficientfusionlayer_pb_kernel(
     bo_view = bo.rearrange("(i p) -> p i", p=P)
 
     with ExitStack() as pools:
+        pools.enter_context(tc.manual_schedule())
         const = pools.enter_context(tc.tile_pool(name="const", bufs=1))
         keep = pools.enter_context(tc.tile_pool(name="keep", bufs=1))
         weight_rows = pools.enter_context(tc.tile_pool(name="weight_rows", bufs=6))
-        resid_rows = pools.enter_context(tc.tile_pool(name="resid_rows", bufs=4))
         stage_one = pools.enter_context(tc.tile_pool(name="stage_one", bufs=4))
         stage_half = pools.enter_context(tc.tile_pool(name="stage_half", bufs=1))
         work = pools.enter_context(tc.tile_pool(name="work", bufs=2))
@@ -52,8 +54,29 @@ def tile_efficientfusionlayer_pb_kernel(
         psum_chain = pools.enter_context(tc.psum_pool(name="psum_chain", bufs=4))
         psum_back = pools.enter_context(tc.psum_pool(name="psum_back", bufs=4))
 
+        def load_pair(pool, view, j, name):
+            rows = pool.tile([P, 2, SIZE], BF16, tag=name)
+            nc.sync.dma_start(out=rows[:], in_=view[:, j])
+            return rows
+
+        def empty_bank(turn, out_ap, bank, scale, bias_col):
+            if turn % VECTOR_TURN == VECTOR_TURN - 1:
+                nc.vector.tensor_scalar(
+                    out=out_ap, in0=bank, scalar1=scale, scalar2=bias_col, op0=ALU.mult, op1=ALU.add
+                )
+            else:
+                nc.scalar.activation(
+                    out=out_ap, in_=bank, func=ACT.Identity, bias=bias_col, scale=scale
+                )
+
+        x_rows = [load_pair(weight_rows, x_view, k, "rows") for k in range(2)]
+
         ident = const.tile([P, P], F32)
         make_identity(nc, ident[:])
+        ident_bf = const.tile([P, P], BF16)
+        make_identity(nc, ident_bf[:])
+        ones_bf = const.tile([P, P], BF16)
+        nc.vector.memset(ones_bf[:], 1.0)
         eps_col = const.tile([P, 1], F32)
         nc.vector.memset(eps_col[:], EPS)
         warm = const.tile([P, 1], F32)
@@ -64,17 +87,34 @@ def tile_efficientfusionlayer_pb_kernel(
         bo_raw = const.tile([P, TILES], BF16)
         with nc.allow_non_contiguous_dma(reason="1024 bias values, one to a partition"):
             nc.scalar.dma_start(out=bo_raw[:], in_=bo_view)
+        norm_rows = const.tile([P, 2, SIZE], BF16)
+        nc.vector.memset(norm_rows[:].bitcast(I32), 0)
+        nc.scalar.dma_start(out=norm_rows[0:1, 0, :], in_=g.unsqueeze(0))
+        nc.scalar.dma_start(out=norm_rows[0:1, 1, :], in_=be.unsqueeze(0))
+
+        def convert_biases():
+            nc.vector.tensor_copy(out=bv_col[:], in_=bv_raw[:])
+            nc.vector.tensor_scalar(
+                out=half_bo_col[:], in0=bo_raw[:], scalar1=0.5, scalar2=None, op0=ALU.mult
+            )
+
+        def spread_norm_rows():
+            for v in range(2):
+                for k in range(2):
+                    cols = slice(k * HALF, (k + 1) * HALF)
+                    spread = psum_back.tile([P, HALF], F32, tag="back")
+                    nc.tensor.matmul(
+                        out=spread[:], lhsT=ones_bf[:], rhs=norm_rows[:, v, cols], start=True, stop=True
+                    )
+                    nc.vector.tensor_copy(out=norm_all[:, v, cols], in_=spread[:])
+
         bv_col = const.tile([P, TILES], F32)
-        nc.vector.tensor_copy(out=bv_col[:], in_=bv_raw[:])
-        bo_col = const.tile([P, TILES], F32)
-        nc.vector.tensor_copy(out=bo_col[:], in_=bo_raw[:])
+        half_bo_col = const.tile([P, TILES], F32)
+        norm_all = const.tile([P, 2, SIZE], BF16)
+        g_all = norm_all[:, 0, :]
+        be_all = norm_all[:, 1, :]
 
-        def load_pair(pool, view, j):
-            rows = pool.tile([P, 2, SIZE], BF16, tag="rows")
-            nc.sync.dma_start(out=rows[:], in_=view[:, j])
-            return rows
-
-        def quantise_transposed(stage, row_tiles, name):
+        def transpose_rows(stage, row_tiles, first_turn, vector_helps):
             n_rows = P * len(row_tiles)
             grouped = stage.tile([P, PASSES, n_rows, PACK], BF16, tag="grouped", align_bytes=64)
             grouped_words = grouped[:].bitcast(F32)
@@ -85,10 +125,16 @@ def tile_efficientfusionlayer_pb_kernel(
                     for u in range(2):
                         first = (2 * c + u) * P
                         nc.tensor.transpose(turned[:, c, u, :], words[:, first : first + P], ident[:])
-                nc.scalar.copy(
-                    out=grouped_words[:, :, n * P : (n + 1) * P, :],
-                    in_=turned[:].rearrange("p c u r -> p c r u"),
-                )
+                copy_out = grouped_words[:, :, n * P : (n + 1) * P, :]
+                copy_in = turned[:].rearrange("p c u r -> p c r u")
+                if vector_helps and (first_turn + n) % VECTOR_TURN == VECTOR_TURN - 1:
+                    nc.vector.tensor_copy(out=copy_out, in_=copy_in)
+                else:
+                    nc.scalar.copy(out=copy_out, in_=copy_in)
+            return grouped
+
+        def quantise(grouped, name):
+            n_rows = grouped.shape[2]
             codes = keep.tile([P, PASSES, n_rows], U32, name=name + "_codes", align_bytes=64)
             scales = keep.tile([P, PASSES, n_rows], U8, name=name + "_scales", align_bytes=64)
             nc.vector.quantize_mx(
@@ -110,32 +156,27 @@ def tile_efficientfusionlayer_pb_kernel(
                     stop=(c == PASSES - 1),
                 )
 
-        def quantise_weight(view, name):
-            quantised = []
-            for j in range(PAIRS):
-                rows = load_pair(weight_rows, view, j)
+        def quantise_weight(view, name, pairs, quantised, vector_helps):
+            waiting = None
+            for j in pairs:
+                rows = load_pair(weight_rows, view, j, "rows")
                 for e in range(2):
-                    tile_name = "%s%d" % (name, 2 * j + e)
-                    quantised.append(quantise_transposed(stage_one, [rows[:, e, :]], tile_name))
-            return quantised
+                    grouped = transpose_rows(stage_one, [rows[:, e, :]], 2 * j + e, vector_helps)
+                    if waiting is not None:
+                        quantised.append(quantise(waiting, "%s%d" % (name, len(quantised))))
+                    waiting = grouped
+            quantised.append(quantise(waiting, "%s%d" % (name, len(quantised))))
 
-        def quantise_batch_half(h):
-            pairs = [load_pair(weight_rows, x_view, 2 * h + k) for k in range(2)]
-            row_tiles = [rows[:, e, :] for rows in pairs for e in range(2)]
-            return quantise_transposed(stage_half, row_tiles, "x%d" % h)
-
-        def value_pass(x_q, val_q, c):
+        def value_products(x_q, c, vector_helps):
             planes = work.tile([P, PACK, HALF], BF16, tag="planes")
             for t in range(PACK):
                 acc = psum_chain.tile([P, HALF], F32, tag="chain")
                 mx_product(acc[:], wv_q[PACK * c + t], x_q)
-                nc.scalar.activation(
-                    out=planes[:, t, :],
-                    in_=acc[:],
-                    func=ACT.Identity,
-                    bias=bv_col[:, PACK * c + t : PACK * c + t + 1],
-                    scale=1.0,
-                )
+                bias_col = bv_col[:, PACK * c + t : PACK * c + t + 1]
+                empty_bank(t if vector_helps else 0, planes[:, t, :], acc[:], 1.0, bias_col)
+            return planes
+
+        def value_quantise(planes, val_q, c):
             grouped = work.tile([P, HALF, PACK], BF16, tag="val_grouped", align_bytes=64)
             nc.vector.tensor_copy(
                 out=grouped[:].rearrange("p (n i) t -> p n t i", i=4),
@@ -152,52 +193,50 @@ def tile_efficientfusionlayer_pb_kernel(
             scales = keep.tile([P, PASSES, HALF], U8, name="val%d_scales" % h, align_bytes=64)
             return codes, scales
 
-        def cross_transposed(val_q, h):
-            cross_t = keep.tile([P, TILES, HALF], F32, name="cross_t%d" % h)
-            for i in range(TILES):
+        def cross_products(val_q, cross_t, tiles, vector_helps):
+            for i in tiles:
                 acc = psum_chain.tile([P, HALF], F32, tag="chain")
                 mx_product(acc[:], wo_q[i], val_q)
-                nc.scalar.activation(
-                    out=cross_t[:, i, :],
-                    in_=acc[:],
-                    func=ACT.Identity,
-                    bias=bo_col[:, i : i + 1],
-                    scale=1.0,
+                empty_bank(
+                    i if vector_helps else 0, cross_t[:, i, :], acc[:], 0.5, half_bo_col[:, i : i + 1]
                 )
-            return cross_t
 
-        y = []
-
-        def residual_pair(j):
-            feat_rows = load_pair(resid_rows, feat_view, j)
-            own_rows = load_pair(resid_rows, own_view, j)
-            for e in range(2):
-                y_tile = keep.tile([P, SIZE], F32, name="y%d" % (2 * j + e))
-                nc.vector.scalar_tensor_tensor(
-                    out=y_tile[:],
-                    in0=own_rows[:, e, :],
-                    scalar=0.5,
-                    in1=feat_rows[:, e, :],
-                    op0=ALU.mult,
-                    op1=ALU.add,
-                )
-                y.append(y_tile)
-
-        def centre(t, cross_t):
+        def gather(t, cross_t):
             first = (t % HALF_TILES) * P
-            sums = small.tile([P, 2], F32, tag="sums")
+            feat_rows = resid[t // 2][0][:, t % 2, :]
+            banks = []
             for k in range(2):
                 back = psum_back.tile([P, BANK_BLOCKS, P], F32, tag="back")
+                nc.tensor.matmul(
+                    out=back[:].rearrange("p n r -> p (n r)"),
+                    lhsT=ident_bf[:],
+                    rhs=feat_rows[:, k * HALF : (k + 1) * HALF],
+                    start=True,
+                    stop=False,
+                )
                 for n in range(BANK_BLOCKS):
-                    nc.tensor.transpose(
-                        back[:, n, :], cross_t[:, BANK_BLOCKS * k + n, first : first + P], ident[:]
+                    nc.tensor.matmul(
+                        out=back[:, n, :],
+                        lhsT=cross_t[:, BANK_BLOCKS * k + n, first : first + P],
+                        rhs=ident[:],
+                        is_transpose=True,
+                        start=False,
+                        stop=(n == BANK_BLOCKS - 1),
                     )
+                banks.append(back)
+            return banks
+
+        def centre(t, banks):
+            own_rows = resid[t // 2][1][:, t % 2, :]
+            y = work.tile([P, SIZE], F32, tag="y")
+            sums = small.tile([P, 2], F32, tag="sums")
+            for k in range(2):
                 cols = slice(k * HALF, (k + 1) * HALF)
                 nc.vector.scalar_tensor_tensor(
-                    out=y[t][:, cols],
-                    in0=back[:].rearrange("p n r -> p (n r)"),
+                    out=y[:, cols],
+                    in0=own_rows[:, cols],
                     scalar=0.5,
-                    in1=y[t][:, cols],
+                    in1=banks[k][:].rearrange("p n r -> p (n r)"),
                     op0=ALU.mult,
                     op1=ALU.add,
                     accum_out=sums[:, k : k + 1],
@@ -215,7 +254,7 @@ def tile_efficientfusionlayer_pb_kernel(
             sum_sq = small.tile([P, 1], F32, tag="sum_sq")
             nc.scalar.activation(
                 out=squares[:],
-                in_=y[t][:],
+                in_=y[:],
                 func=ACT.Square,
                 bias=neg_mean[:],
                 scale=1.0,
@@ -227,12 +266,7 @@ def tile_efficientfusionlayer_pb_kernel(
             )
             result = normed.tile([P, SIZE], F32, tag="result")
             nc.vector.scalar_tensor_tensor(
-                out=result[:],
-                in0=y[t][:],
-                scalar=neg_mean[:],
-                in1=g_all[:],
-                op0=ALU.add,
-                op1=ALU.mult,
+                out=result[:], in0=y[:], scalar=neg_mean[:], in1=g_all, op0=ALU.add, op1=ALU.mult
             )
             return result, std
 
@@ -241,44 +275,57 @@ def tile_efficientfusionlayer_pb_kernel(
             rstd = small.tile([P, 1], F32, tag="rstd")
             nc.vector.reciprocal(out=rstd[:], in_=std[:])
             nc.vector.scalar_tensor_tensor(
-                out=result[:],
-                in0=result[:],
-                scalar=rstd[:],
-                in1=be_all[:],
-                op0=ALU.mult,
-                op1=ALU.add,
+                out=result[:], in0=result[:], scalar=rstd[:], in1=be_all, op0=ALU.mult, op1=ALU.add
             )
             nc.sync.dma_start(out=out_view[:, t, :], in_=result[:])
 
-        x_q0 = quantise_batch_half(0)
-        wv_q = quantise_weight(wv_view, "wv")
-        val_q0 = new_val(0)
-        for c in range(PASSES):
-            value_pass(x_q0, val_q0, c)
-        wo_q = quantise_weight(wo_view, "wo")
-        g_all = const.tile([P, SIZE], BF16)
-        nc.sync.dma_start(out=g_all[:], in_=g.partition_broadcast(P))
-        be_all = const.tile([P, SIZE], BF16)
-        nc.sync.dma_start(out=be_all[:], in_=be.partition_broadcast(P))
-        residual_pair(0)
-        residual_pair(1)
-        cross_t0 = cross_transposed(val_q0, 0)
+        def load_resid(j):
+            return load_pair(keep, feat_view, j, "feat%d" % j), load_pair(keep, own_view, j, "own%d" % j)
 
-        x_q1 = quantise_batch_half(1)
-        residual_pair(2)
-        residual_pair(3)
+        def halves(rows_list):
+            return [rows[:, e, :] for rows in rows_list for e in range(2)]
+
+        x_grouped = transpose_rows(stage_half, halves(x_rows), 0, True)
+        x_q0 = quantise(x_grouped, "x0")
+        convert_biases()
+        wv_q = []
+        quantise_weight(wv_view, "wv", range(0, 2), wv_q, True)
+        val_q0 = new_val(0)
+        wo_q = []
+        planes0 = value_products(x_q0, 0, True)
+        quantise_weight(wv_view, "wv", range(2, 4), wv_q, True)
+        value_quantise(planes0, val_q0, 0)
+        planes1 = value_products(x_q0, 1, True)
+        quantise_weight(wo_view, "wo", range(0, 1), wo_q, False)
+        value_quantise(planes1, val_q0, 1)
+        quantise_weight(wo_view, "wo", range(1, 4), wo_q, False)
+        x_rows = [load_pair(weight_rows, x_view, 2 + k, "rows") for k in range(2)]
+        resid = [load_resid(j) for j in range(PAIRS)]
+        spread_norm_rows()
+        cross_t0 = keep.tile([P, TILES, HALF], F32, name="cross_t0")
+        cross_products(val_q0, cross_t0, range(TILES), True)
+
         val_q1 = new_val(1)
-        centred = centre(0, cross_t0)
-        value_pass(x_q1, val_q1, 0)
-        previous, centred = centred, centre(1, cross_t0)
+        cross_t1 = keep.tile([P, TILES, HALF], F32, name="cross_t1")
+        banks = [gather(0, cross_t0), gather(1, cross_t0)]
+        x_grouped = transpose_rows(stage_half, halves(x_rows), 0, False)
+        centred = centre(0, banks[0])
+        x_q1 = quantise(x_grouped, "x1")
+        planes0 = value_products(x_q1, 0, False)
+        banks.append(gather(2, cross_t0))
+        planes1 = value_products(x_q1, 1, False)
+        previous, centred = centred, centre(1, banks[1])
         finish(0, previous)
-        value_pass(x_q1, val_q1, 1)
-        previous, centred = centred, centre(2, cross_t0)
+        value_quantise(planes0, val_q1, 0)
+        banks.append(gather(3, cross_t0))
+        previous, centred = centred, centre(2, banks[2])
+        value_quantise(planes1, val_q1, 1)
         finish(1, previous)
-        cross_t1 = cross_transposed(val_q1, 1)
-        previous, centred = centred, centre(3, cross_t0)
+        cross_products(val_q1, cross_t1, range(TILES), False)
+        previous, centred = centred, centre(3, banks[3])
         finish(2, previous)
         for t in range(HALF_TILES, TILES):
-            previous, centred = centred, centre(t, cross_t1)
+            banks.append(gather(t, cross_t1))
+            previous, centred = centred, centre(t, banks[t])
             finish(t - 1, previous)
         finish(TILES - 1, centred)

@@ -42,7 +42,6 @@ def tile_efficientfusionlayer_pb_kernel(
     bo_view = bo.rearrange("(i p) -> p i", p=P)
 
     with ExitStack() as pools:
-        pools.enter_context(tc.manual_schedule())
         const = pools.enter_context(tc.tile_pool(name="const", bufs=1))
         keep = pools.enter_context(tc.tile_pool(name="keep", bufs=1))
         weight_rows = pools.enter_context(tc.tile_pool(name="weight_rows", bufs=6))
@@ -69,6 +68,15 @@ def tile_efficientfusionlayer_pb_kernel(
                     out=out_ap, in_=bank, func=ACT.Identity, bias=bias_col, scale=scale
                 )
 
+        norm_rows = const.tile([P, 2, SIZE], BF16)
+        nc.vector.memset(norm_rows[:].bitcast(I32), 0)
+        nc.sync.dma_start(out=norm_rows[0:1, 0, :], in_=g.unsqueeze(0))
+        nc.sync.dma_start(out=norm_rows[0:1, 1, :], in_=be.unsqueeze(0))
+        bv_raw = const.tile([P, TILES], BF16)
+        nc.sync.dma_start(out=bv_raw[:].rearrange("p (j e) -> p j e", e=2), in_=bv_view)
+        bo_raw = const.tile([P, TILES], BF16)
+        with nc.allow_non_contiguous_dma(reason="1024 bias values, one to a partition"):
+            nc.sync.dma_start(out=bo_raw[:], in_=bo_view)
         x_rows = [load_pair(weight_rows, x_view, k, "rows") for k in range(2)]
 
         ident = const.tile([P, P], F32)
@@ -82,15 +90,6 @@ def tile_efficientfusionlayer_pb_kernel(
         warm = const.tile([P, 1], F32)
         nc.scalar.activation(out=warm[:], in_=eps_col[:], func=ACT.Sqrt)
 
-        bv_raw = const.tile([P, TILES], BF16)
-        nc.scalar.dma_start(out=bv_raw[:].rearrange("p (j e) -> p j e", e=2), in_=bv_view)
-        bo_raw = const.tile([P, TILES], BF16)
-        with nc.allow_non_contiguous_dma(reason="1024 bias values, one to a partition"):
-            nc.scalar.dma_start(out=bo_raw[:], in_=bo_view)
-        norm_rows = const.tile([P, 2, SIZE], BF16)
-        nc.vector.memset(norm_rows[:].bitcast(I32), 0)
-        nc.scalar.dma_start(out=norm_rows[0:1, 0, :], in_=g.unsqueeze(0))
-        nc.scalar.dma_start(out=norm_rows[0:1, 1, :], in_=be.unsqueeze(0))
 
         def convert_biases():
             nc.vector.tensor_copy(out=bv_col[:], in_=bv_raw[:])

from contextlib import ExitStack

import concourse.mybir as mybir
from concourse.masks import make_identity

BF16 = mybir.dt.bfloat16
F32 = mybir.dt.float32
I32 = mybir.dt.int32
U32 = mybir.dt.uint32
U8 = mybir.dt.uint8
FP8X4 = mybir.dt.float8_e4m3fn_x4
ACT = mybir.ActivationFunctionType
ALU = mybir.AluOpType

P = 128
SIZE = 1024
PACK = 4
PASSES = SIZE // (P * PACK)
TILES = SIZE // P
PAIRS = TILES // 2
HALF = 512
HALF_TILES = HALF // P
BANK_BLOCKS = HALF // P
VECTOR_TURN = 4
EPS = 1e-5

FLOPS = 2 * 2 * SIZE * SIZE * SIZE


def tile_efficientfusionlayer_pb_kernel(
    tc, feat, own_self, other_self, Wv, bv, Wo, bo, g, be, out
):
    nc = tc.nc

    x_view = other_self.rearrange("(p j e) d -> p j e d", j=PAIRS, e=2)
    feat_view = feat.rearrange("(p j e) d -> p j e d", j=PAIRS, e=2)
    own_view = own_self.rearrange("(p j e) d -> p j e d", j=PAIRS, e=2)
    out_view = out.rearrange("(p t) d -> p t d", t=TILES)
    wv_view = Wv.rearrange("(j p e) d -> p j e d", j=PAIRS, e=2)
    bv_view = bv.rearrange("(j p e) -> p j e", j=PAIRS, e=2)
    wo_view = Wo.rearrange("(j e p) v -> p j e v", j=PAIRS, e=2)
    bo_view = bo.rearrange("(i p) -> p i", p=P)

    with ExitStack() as pools:
        const = pools.enter_context(tc.tile_pool(name="const", bufs=1))
        keep = pools.enter_context(tc.tile_pool(name="keep", bufs=1))
        weight_rows = pools.enter_context(tc.tile_pool(name="weight_rows", bufs=6))
        stage_one = pools.enter_context(tc.tile_pool(name="stage_one", bufs=4))
        stage_half = pools.enter_context(tc.tile_pool(name="stage_half", bufs=1))
        work = pools.enter_context(tc.tile_pool(name="work", bufs=2))
        normed = pools.enter_context(tc.tile_pool(name="normed", bufs=3))
        small = pools.enter_context(tc.tile_pool(name="small", bufs=3))
        psum_chain = pools.enter_context(tc.psum_pool(name="psum_chain", bufs=4))
        psum_back = pools.enter_context(tc.psum_pool(name="psum_back", bufs=4))

        def load_pair(pool, view, j, name):
            rows = pool.tile([P, 2, SIZE], BF16, tag=name)
            nc.sync.dma_start(out=rows[:], in_=view[:, j])
            return rows

        def empty_bank(turn, out_ap, bank, scale, bias_col):
            if turn % VECTOR_TURN == VECTOR_TURN - 1:
                nc.vector.tensor_scalar(
                    out=out_ap, in0=bank, scalar1=scale, scalar2=bias_col, op0=ALU.mult, op1=ALU.add
                )
            else:
                nc.scalar.activation(
                    out=out_ap, in_=bank, func=ACT.Identity, bias=bias_col, scale=scale
                )

        norm_rows = const.tile([P, 2, SIZE], BF16)
        nc.vector.memset(norm_rows[:].bitcast(I32), 0)
        nc.sync.dma_start(out=norm_rows[0:1, 0, :], in_=g.unsqueeze(0))
        nc.sync.dma_start(out=norm_rows[0:1, 1, :], in_=be.unsqueeze(0))
        bv_raw = const.tile([P, TILES], BF16)
        nc.sync.dma_start(out=bv_raw[:].rearrange("p (j e) -> p j e", e=2), in_=bv_view)
        bo_raw = const.tile([P, TILES], BF16)
        with nc.allow_non_contiguous_dma(reason="1024 bias values, one to a partition"):
            nc.sync.dma_start(out=bo_raw[:], in_=bo_view)
        x_rows = [load_pair(weight_rows, x_view, k, "rows") for k in range(2)]

        ident = const.tile([P, P], F32)
        make_identity(nc, ident[:])
        ident_bf = const.tile([P, P], BF16)
        make_identity(nc, ident_bf[:])
        ones_bf = const.tile([P, P], BF16)
        nc.vector.memset(ones_bf[:], 1.0)
        eps_col = const.tile([P, 1], F32)
        nc.vector.memset(eps_col[:], EPS)
        warm = const.tile([P, 1], F32)
        nc.scalar.activation(out=warm[:], in_=eps_col[:], func=ACT.Sqrt)


        def convert_biases():
            nc.vector.tensor_copy(out=bv_col[:], in_=bv_raw[:])
            nc.vector.tensor_scalar(
                out=half_bo_col[:], in0=bo_raw[:], scalar1=0.5, scalar2=None, op0=ALU.mult
            )

        def spread_norm_rows():
            for v in range(2):
                for k in range(2):
                    cols = slice(k * HALF, (k + 1) * HALF)
                    spread = psum_back.tile([P, HALF], F32, tag="back")
                    nc.tensor.matmul(
                        out=spread[:], lhsT=ones_bf[:], rhs=norm_rows[:, v, cols], start=True, stop=True
                    )
                    nc.vector.tensor_copy(out=norm_all[:, v, cols], in_=spread[:])

        bv_col = const.tile([P, TILES], F32)
        half_bo_col = const.tile([P, TILES], F32)
        norm_all = const.tile([P, 2, SIZE], BF16)
        g_all = norm_all[:, 0, :]
        be_all = norm_all[:, 1, :]

        def transpose_rows(stage, row_tiles, first_turn, vector_helps):
            n_rows = P * len(row_tiles)
            grouped = stage.tile([P, PASSES, n_rows, PACK], BF16, tag="grouped", align_bytes=64)
            grouped_words = grouped[:].bitcast(F32)
            for n, rows in enumerate(row_tiles):
                words = rows.bitcast(F32)
                turned = psum_chain.tile([P, PASSES, 2, P], F32, tag="chain")
                for c in range(PASSES):
                    for u in range(2):
                        first = (2 * c + u) * P
                        nc.tensor.transpose(turned[:, c, u, :], words[:, first : first + P], ident[:])
                copy_out = grouped_words[:, :, n * P : (n + 1) * P, :]
                copy_in = turned[:].rearrange("p c u r -> p c r u")
                if vector_helps and (first_turn + n) % VECTOR_TURN == VECTOR_TURN - 1:
                    nc.vector.tensor_copy(out=copy_out, in_=copy_in)
                else:
                    nc.scalar.copy(out=copy_out, in_=copy_in)
            return grouped

        def quantise(grouped, name):
            n_rows = grouped.shape[2]
            codes = keep.tile([P, PASSES, n_rows], U32, name=name + "_codes", align_bytes=64)
            scales = keep.tile([P, PASSES, n_rows], U8, name=name + "_scales", align_bytes=64)
            nc.vector.quantize_mx(
                out=codes[:].rearrange("p c r -> p (c r)").bitcast(FP8X4),
                scales=scales[:].rearrange("p c r -> p (c r)"),
                in_=grouped[:].rearrange("p c r t -> p (c r t)"),
            )
            return codes, scales

        def mx_product(acc, stationary, moving):
            for c in range(PASSES):
                nc.tensor.matmul_mx(
                    out=acc,
                    lhsT=stationary[0][:, c, :].bitcast(FP8X4),
                    lhsT_scale=stationary[1][:, c, :],
                    rhs=moving[0][:, c, :].bitcast(FP8X4),
                    rhs_scale=moving[1][:, c, :],
                    start=(c == 0),
                    stop=(c == PASSES - 1),
                )

        def quantise_weight(view, name, pairs, quantised, vector_helps):
            waiting = None
            for j in pairs:
                rows = load_pair(weight_rows, view, j, "rows")
                for e in range(2):
                    grouped = transpose_rows(stage_one, [rows[:, e, :]], 2 * j + e, vector_helps)
                    if waiting is not None:
                        quantised.append(quantise(waiting, "%s%d" % (name, len(quantised))))
                    waiting = grouped
            quantised.append(quantise(waiting, "%s%d" % (name, len(quantised))))

        def value_products(x_q, c, vector_helps):
            planes = work.tile([P, PACK, HALF], BF16, tag="planes")
            for t in range(PACK):
                acc = psum_chain.tile([P, HALF], F32, tag="chain")
                mx_product(acc[:], wv_q[PACK * c + t], x_q)
                bias_col = bv_col[:, PACK * c + t : PACK * c + t + 1]
                empty_bank(t if vector_helps else 0, planes[:, t, :], acc[:], 1.0, bias_col)
            return planes

        def value_quantise(planes, val_q, c):
            grouped = work.tile([P, HALF, PACK], BF16, tag="val_grouped", align_bytes=64)
            nc.vector.tensor_copy(
                out=grouped[:].rearrange("p (n i) t -> p n t i", i=4),
                in_=planes[:].rearrange("p t (n i) -> p n t i", i=4),
            )
            nc.vector.quantize_mx(
                out=val_q[0][:, c, :].bitcast(FP8X4),
                scales=val_q[1][:, c, :],
                in_=grouped[:].rearrange("p n t -> p (n t)"),
            )

        def new_val(h):
            codes = keep.tile([P, PASSES, HALF], U32, name="val%d_codes" % h, align_bytes=64)
            scales = keep.tile([P, PASSES, HALF], U8, name="val%d_scales" % h, align_bytes=64)
            return codes, scales

        def cross_products(val_q, cross_t, tiles, vector_helps):
            for i in tiles:
                acc = psum_chain.tile([P, HALF], F32, tag="chain")
                mx_product(acc[:], wo_q[i], val_q)
                empty_bank(
                    i if vector_helps else 0, cross_t[:, i, :], acc[:], 0.5, half_bo_col[:, i : i + 1]
                )

        def gather(t, cross_t):
            first = (t % HALF_TILES) * P
            feat_rows = resid[t // 2][0][:, t % 2, :]
            banks = []
            for k in range(2):
                back = psum_back.tile([P, BANK_BLOCKS, P], F32, tag="back")
                nc.tensor.matmul(
                    out=back[:].rearrange("p n r -> p (n r)"),
                    lhsT=ident_bf[:],
                    rhs=feat_rows[:, k * HALF : (k + 1) * HALF],
                    start=True,
                    stop=False,
                )
                for n in range(BANK_BLOCKS):
                    nc.tensor.matmul(
                        out=back[:, n, :],
                        lhsT=cross_t[:, BANK_BLOCKS * k + n, first : first + P],
                        rhs=ident[:],
                        is_transpose=True,
                        start=False,
                        stop=(n == BANK_BLOCKS - 1),
                    )
                banks.append(back)
            return banks

        def centre(t, banks):
            own_rows = resid[t // 2][1][:, t % 2, :]
            y = work.tile([P, SIZE], F32, tag="y")
            sums = small.tile([P, 2], F32, tag="sums")
            for k in range(2):
                cols = slice(k * HALF, (k + 1) * HALF)
                nc.vector.scalar_tensor_tensor(
                    out=y[:, cols],
                    in0=own_rows[:, cols],
                    scalar=0.5,
                    in1=banks[k][:].rearrange("p n r -> p (n r)"),
                    op0=ALU.mult,
                    op1=ALU.add,
                    accum_out=sums[:, k : k + 1],
                )
            neg_mean = small.tile([P, 1], F32, tag="neg_mean")
            nc.vector.tensor_scalar(
                out=neg_mean[:],
                in0=sums[:, 0:1],
                scalar1=sums[:, 1:2],
                scalar2=-1.0 / SIZE,
                op0=ALU.add,
                op1=ALU.mult,
            )
            squares = work.tile([P, SIZE], BF16, tag="squares")
            sum_sq = small.tile([P, 1], F32, tag="sum_sq")
            nc.scalar.activation(
                out=squares[:],
                in_=y[:],
                func=ACT.Square,
                bias=neg_mean[:],
                scale=1.0,
                accum_out=sum_sq[:],
            )
            std = small.tile([P, 1], F32, tag="std")
            nc.scalar.activation(
                out=std[:], in_=sum_sq[:], func=ACT.Sqrt, bias=eps_col[:], scale=1.0 / SIZE
            )
            result = normed.tile([P, SIZE], F32, tag="result")
            nc.vector.scalar_tensor_tensor(
                out=result[:], in0=y[:], scalar=neg_mean[:], in1=g_all, op0=ALU.add, op1=ALU.mult
            )
            return result, std

        def finish(t, centred):
            result, std = centred
            rstd = small.tile([P, 1], F32, tag="rstd")
            nc.vector.reciprocal(out=rstd[:], in_=std[:])
            nc.vector.scalar_tensor_tensor(
                out=result[:], in0=result[:], scalar=rstd[:], in1=be_all, op0=ALU.mult, op1=ALU.add
            )
            nc.sync.dma_start(out=out_view[:, t, :], in_=result[:])

        def load_resid(j):
            return load_pair(keep, feat_view, j, "feat%d" % j), load_pair(keep, own_view, j, "own%d" % j)

        def halves(rows_list):
            return [rows[:, e, :] for rows in rows_list for e in range(2)]

        x_grouped = transpose_rows(stage_half, halves(x_rows), 0, True)
        x_q0 = quantise(x_grouped, "x0")
        convert_biases()
        wv_q = []
        quantise_weight(wv_view, "wv", range(0, 2), wv_q, True)
        val_q0 = new_val(0)
        wo_q = []
        planes0 = value_products(x_q0, 0, True)
        quantise_weight(wv_view, "wv", range(2, 4), wv_q, True)
        value_quantise(planes0, val_q0, 0)
        planes1 = value_products(x_q0, 1, True)
        quantise_weight(wo_view, "wo", range(0, 1), wo_q, False)
        value_quantise(planes1, val_q0, 1)
        quantise_weight(wo_view, "wo", range(1, 4), wo_q, False)
        x_rows = [load_pair(weight_rows, x_view, 2 + k, "rows") for k in range(2)]
        resid = [load_resid(j) for j in range(PAIRS)]
        spread_norm_rows()
        cross_t0 = keep.tile([P, TILES, HALF], F32, name="cross_t0")
        cross_products(val_q0, cross_t0, range(TILES), True)

        val_q1 = new_val(1)
        cross_t1 = keep.tile([P, TILES, HALF], F32, name="cross_t1")
        banks = [gather(0, cross_t0), gather(1, cross_t0)]
        x_grouped = transpose_rows(stage_half, halves(x_rows), 0, False)
        centred = centre(0, banks[0])
        x_q1 = quantise(x_grouped, "x1")
        planes0 = value_products(x_q1, 0, False)
        banks.append(gather(2, cross_t0))
        planes1 = value_products(x_q1, 1, False)
        previous, centred = centred, centre(1, banks[1])
        finish(0, previous)
        value_quantise(planes0, val_q1, 0)
        banks.append(gather(3, cross_t0))
        previous, centred = centred, centre(2, banks[2])
        value_quantise(planes1, val_q1, 1)
        finish(1, previous)
        cross_products(val_q1, cross_t1, range(TILES), False)
        previous, centred = centred, centre(3, banks[3])
        finish(2, previous)
        for t in range(HALF_TILES, TILES):
            banks.append(gather(t, cross_t1))
            previous, centred = centred, centre(t, banks[t])
            finish(t - 1, previous)
        finish(TILES - 1, centred)
